import numpy as np
import ml_dtypes

BF16 = ml_dtypes.bfloat16


def bf(x):
    return np.asarray(x, np.float32).astype(BF16)


def f32(x):
    return np.asarray(x, np.float32)


def f64(x):
    return np.asarray(x).astype(np.float64)


def striped(idx):
    return np.tile(idx.reshape(-1, 16).T, (8, 1))


D, S, N, L = 512, 4096, 1024, 128
EPS = 1e-8
QK_GAIN = 1.75


def relu(v):
    return np.maximum(v, 0.0)


def setup_inputs():
    sc = 1.0 / np.sqrt(D)
    return {
        "base": f32(np.random.standard_normal((D, S))),
        "x": bf(np.random.standard_normal((D, N))),
        "wq": bf(QK_GAIN * sc * np.random.standard_normal((D, D))),
        "wk": bf(QK_GAIN * sc * np.random.standard_normal((D, D))),
        "wv": bf(sc * np.random.standard_normal((D, D))),
        "bv": f32(0.1 * np.random.standard_normal((D, 1))),
        "w1": bf(sc * np.random.standard_normal((D, D))),
        "b1": f32(0.1 * np.random.standard_normal((D, 1))),
        "w2": bf(sc * np.random.standard_normal((D, D))),
        "b2": f32(0.1 * np.random.standard_normal((D, 1))),
        "gain": f32(1.0 + 0.1 * np.random.standard_normal((D, 1))),
        "shift": f32(0.1 * np.random.standard_normal((D, 1))),
        "offs": striped(np.random.permutation(S)[:N]),
    }


def reference(base, x, wq, wk, wv, bv, w1, b1, w2, b2, gain, shift, offs):
    idx = offs[:16].T.reshape(-1)
    xx = f64(x)
    q = relu(f64(wq).T @ xx)
    k = relu(f64(wk).T @ xx)
    v = relu(f64(wv).T @ xx + f64(bv))
    o = np.zeros_like(xx)
    for u in range(N // L):
        sl = slice(u * L, (u + 1) * L)
        sc = q[:, sl].T @ k[:, sl] / np.sqrt(D)
        e = np.exp(sc - sc.max(axis=1, keepdims=True))
        a = e / e.sum(axis=1, keepdims=True)
        o[:, sl] = v[:, sl] @ a.T
    y = o + xx
    r = relu(f64(w1).T @ y + f64(b1))
    h = f64(w2).T @ r + f64(b2)
    mu = h.mean(axis=0, keepdims=True)
    var = np.square(h - mu).mean(axis=0, keepdims=True)
    z = (h - mu) / np.sqrt(var + EPS) * f64(gain) + f64(shift)
    out = f64(base).copy()
    out[:, idx] = z + y
    return out

@@ -1,0 +1,198 @@
+import math
+
+import concourse.mybir as mybir
+from concourse.masks import make_identity
+
+P = 128
+D = 512
+S = 4096
+N = 1024
+L = 128
+DB = D // P
+CHUNK = 512
+SEQS = CHUNK // L
+EPS = 1e-8
+FLOPS = 2 * 5 * D * D * N + 2 * 2 * (N // L) * L * L * D
+
+BF16, F32, U16 = mybir.dt.bfloat16, mybir.dt.float32, mybir.dt.uint16
+ADD, SUB, MULT = mybir.AluOpType.add, mybir.AluOpType.subtract, mybir.AluOpType.mult
+RELU = mybir.ActivationFunctionType.Relu
+EXP = mybir.ActivationFunctionType.Exp
+SQRT = mybir.ActivationFunctionType.Sqrt
+IDENTITY = mybir.ActivationFunctionType.Identity
+
+
+def tile_scriptwriter_cpre_b_kernel(tc, base, x, wq, wk, wv, bv, w1, b1, w2, b2, gain, shift, offs, out):
+    nc = tc.nc
+    with (
+        tc.tile_pool(name="held", bufs=1) as held,
+        tc.tile_pool(name="work", bufs=2) as work,
+        tc.tile_pool(name="small", bufs=4) as small,
+        tc.psum_pool(name="acc_pool", bufs=4) as acc_pool,
+        tc.psum_pool(name="attn_pool", bufs=1) as attn_pool,
+        tc.psum_pool(name="flip_pool", bufs=2) as flip_pool,
+    ):
+        offsets = held.tile([P, N // 16], U16, name="offsets")
+        nc.sync.dma_start(offsets[:], offs)
+
+        x_sb = held.tile([P, DB, N], BF16, name="x_sb")
+        x_blocks = x.rearrange("(kb p) n -> p kb n", p=P)
+        for kb in range(DB):
+            nc.sync.dma_start(x_sb[:, kb, :], x_blocks[:, kb, :])
+
+        def load_weight(w, name):
+            w_sb = held.tile([P, DB, D], BF16, name=name)
+            nc.sync.dma_start(w_sb[:], w.rearrange("(kb p) m -> p kb m", p=P))
+            return w_sb
+
+        def load_along_free_axis(vec, name):
+            vec_all = held.tile([P, D], F32, name=name)
+            nc.sync.dma_start(vec_all[:], vec.rearrange("d one -> (d one)").partition_broadcast(P))
+            return vec_all
+
+        wq_sb = load_weight(wq, "wq_sb")
+        wk_sb = load_weight(wk, "wk_sb")
+        wv_sb = load_weight(wv, "wv_sb")
+        bv_all = load_along_free_axis(bv, "bv_all")
+
+        rows = held.tile([P, P], F32, name="rows")
+        nc.vector.memset(rows[:], 0.0)
+        for i, vec in enumerate((b1, gain, shift)):
+            nc.sync.dma_start(rows[i * DB : (i + 1) * DB, :], vec.rearrange("(b p) one -> b (p one)", p=P))
+
+        w1_sb = load_weight(w1, "w1_sb")
+        w2_sb = load_weight(w2, "w2_sb")
+        b2_all = load_along_free_axis(b2, "b2_all")
+
+        windows = [held.tile([P, S], F32, name=f"window{b}") for b in range(DB)]
+        for b in range(DB):
+            nc.sync.dma_start(windows[b][:], base[b * P : (b + 1) * P, :])
+
+        ident_f = held.tile([P, P], F32, name="ident_f")
+        make_identity(nc, ident_f[:])
+        ident_b = held.tile([P, P], BF16, name="ident_b")
+        make_identity(nc, ident_b[:])
+        eps_col = held.tile([P, 1], F32, name="eps_col")
+        nc.vector.memset(eps_col[:], EPS)
+
+        flipped = flip_pool.tile([P, DB, P], F32, name="flipped")
+        nc.tensor.transpose(flipped[:, 0, :], rows[:], ident_f[:])
+        cols = held.tile([P, 3 * DB], F32, name="cols")
+        nc.vector.tensor_copy(cols[:], flipped[:, 0, 0 : 3 * DB])
+        b1_col = [cols[:, b : b + 1] for b in range(DB)]
+        gain_col = [cols[:, DB + b : DB + b + 1] for b in range(DB)]
+        shift_col = [cols[:, 2 * DB + b : 2 * DB + b + 1] for b in range(DB)]
+
+        q_sb = held.tile([P, DB, N], BF16, name="q_sb")
+        k_sb = held.tile([P, DB, N], BF16, name="k_sb")
+        vt_sb = held.tile([P, N // L, D], BF16, name="vt_sb")
+        y_bf = held.tile([P, DB, N], BF16, name="y_bf")
+        r_sb = held.tile([P, DB, N], BF16, name="r_sb")
+        y_sb = [held.tile([P, N], F32, name=f"y{b}") for b in range(DB)]
+        z_sb = [held.tile([P, N], F32, name=f"z{b}") for b in range(DB)]
+
+        def block(i):
+            return slice(i * P, (i + 1) * P)
+
+        def project_qk(c):
+            chunk = slice(c * CHUNK, (c + 1) * CHUNK)
+            for m in range(DB):
+                acc = acc_pool.tile([P, CHUNK], F32, name="acc")
+                for kb in range(DB):
+                    nc.tensor.matmul(acc[:], wq_sb[:, kb, block(m)], x_sb[:, kb, chunk], start=(kb == 0), stop=(kb == DB - 1))
+                nc.scalar.activation(q_sb[:, m, chunk], acc[:], RELU)
+            for m in range(DB):
+                acc = acc_pool.tile([P, CHUNK], F32, name="acc")
+                for kb in range(DB):
+                    nc.tensor.matmul(acc[:], wk_sb[:, kb, block(m)], x_sb[:, kb, chunk], start=(kb == 0), stop=(kb == DB - 1))
+                nc.vector.tensor_scalar_max(k_sb[:, m, chunk], acc[:], 0.0)
+
+        def project_v(c):
+            for u in range(c * SEQS, (c + 1) * SEQS):
+                acc = acc_pool.tile([P, D], F32, name="acc")
+                for kb in range(DB):
+                    nc.tensor.matmul(acc[:], x_sb[:, kb, block(u)], wv_sb[:, kb, :], start=(kb == 0), stop=(kb == DB - 1))
+                v_pre = work.tile([P, D], F32, name="v_pre")
+                nc.vector.tensor_tensor(v_pre[:], acc[:], bv_all[:], ADD)
+                nc.gpsimd.tensor_scalar_max(vt_sb[:, u, :], v_pre[:], 0.0)
+
+        def attention_weights(c):
+            scores = attn_pool.tile([P, SEQS, L], F32, name="scores")
+            for s in range(SEQS):
+                u = c * SEQS + s
+                for m in range(DB):
+                    nc.tensor.matmul(scores[:, s, :], q_sb[:, m, block(u)], k_sb[:, m, block(u)], start=(m == 0), stop=(m == DB - 1))
+            top = small.tile([P, SEQS], F32, name="top")
+            nc.vector.reduce_max(top[:], scores[:], mybir.AxisListType.X)
+            neg_top = small.tile([P, SEQS], F32, name="neg_top")
+            nc.vector.tensor_scalar_mul(neg_top[:], top[:], -1.0 / math.sqrt(D))
+            e = work.tile([P, SEQS, L], F32, name="e")
+            sums = small.tile([P, SEQS], F32, name="sums")
+            for s in range(SEQS):
+                nc.scalar.activation(
+                    e[:, s, :], scores[:, s, :], EXP, bias=neg_top[:, s : s + 1], scale=1.0 / math.sqrt(D),
+                    accum_out=sums[:, s : s + 1],
+                )
+            inv_sums = small.tile([P, SEQS], F32, name="inv_sums")
+            nc.vector.reciprocal(inv_sums[:], sums[:])
+            a_bf = work.tile([P, SEQS, L], BF16, name="a_bf")
+            for s in range(SEQS):
+                nc.vector.tensor_scalar_mul(a_bf[:, s, :], e[:, s, :], inv_sums[:, s : s + 1])
+            at_ps = attn_pool.tile([P, SEQS, L], BF16, name="at_ps")
+            for s in range(SEQS):
+                nc.tensor.transpose(at_ps[:, s, :], a_bf[:, s, :], ident_b[:])
+            at_sb = work.tile([P, SEQS, L], BF16, name="at_sb")
+            nc.vector.tensor_copy(at_sb[:], at_ps[:])
+            return at_sb
+
+        def attend(c, at_sb):
+            chunk = slice(c * CHUNK, (c + 1) * CHUNK)
+            for b in range(DB):
+                acc = acc_pool.tile([P, CHUNK], F32, name="acc")
+                for s in range(SEQS):
+                    nc.tensor.matmul(acc[:, block(s)], vt_sb[:, c * SEQS + s, block(b)], at_sb[:, s, :], start=True, stop=True)
+                nc.vector.tensor_tensor(y_sb[b][:, chunk], acc[:], x_sb[:, b, chunk], ADD)
+                nc.gpsimd.tensor_copy(y_bf[:, b, chunk], y_sb[b][:, chunk])
+
+        def feed_forward_hidden(c):
+            chunk = slice(c * CHUNK, (c + 1) * CHUNK)
+            for m in range(DB):
+                acc = acc_pool.tile([P, CHUNK], F32, name="acc")
+                for kb in range(DB):
+                    nc.tensor.matmul(acc[:], w1_sb[:, kb, block(m)], y_bf[:, kb, chunk], start=(kb == 0), stop=(kb == DB - 1))
+                nc.scalar.activation(r_sb[:, m, chunk], acc[:], RELU, bias=b1_col[m])
+
+        def feed_forward_out_and_norm(c):
+            for u in range(c * SEQS, (c + 1) * SEQS):
+                acc = acc_pool.tile([P, D], F32, name="acc")
+                for eb in range(DB):
+                    nc.tensor.matmul(acc[:], r_sb[:, eb, block(u)], w2_sb[:, eb, :], start=(eb == 0), stop=(eb == DB - 1))
+                h = work.tile([P, D], F32, name="h")
+                nc.vector.tensor_tensor(h[:], acc[:], b2_all[:], ADD)
+                stats = small.tile([P, 6], F32, name="stats")
+                nc.vector.bn_stats(stats[:], h[:])
+                mean_var = small.tile([P, 2], F32, name="mean_var")
+                nc.vector.bn_aggr(mean_var[:], stats[:])
+                std = small.tile([P, 1], F32, name="std")
+                nc.scalar.activation(std[:], mean_var[:, 1:2], SQRT, bias=eps_col[:])
+                inv_std = small.tile([P, 1], F32, name="inv_std")
+                nc.vector.reciprocal(inv_std[:], std[:])
+                normed = work.tile([P, D], F32, name="normed")
+                nc.vector.tensor_scalar(normed[:], h[:], mean_var[:, 0:1], inv_std[:], SUB, MULT)
+                flipped = flip_pool.tile([P, DB, P], F32, name="flipped")
+                for b in range(DB):
+                    nc.tensor.transpose(flipped[:, b, :], normed[:, block(b)], ident_f[:])
+                for b in range(DB):
+                    nc.scalar.activation(z_sb[b][:, block(u)], flipped[:, b, :], IDENTITY, bias=shift_col[b], scale=gain_col[b])
+
+        for c in range(N // CHUNK):
+            project_qk(c)
+            project_v(c)
+            at_sb = attention_weights(c)
+            attend(c, at_sb)
+            feed_forward_hidden(c)
+            feed_forward_out_and_norm(c)
+
+        for b in range(DB):
+            nc.vector.tensor_tensor(windows[b][:].indirect(offsets[:]), z_sb[b][:], y_sb[b][:], ADD)
+            nc.sync.dma_start(out[b * P : (b + 1) * P, :], windows[b][:])

@@ -11,6 +11,7 @@ L = 128
 DB = D // P
 CHUNK = 512
 SEQS = CHUNK // L
+LAG = 2
 EPS = 1e-8
 FLOPS = 2 * 5 * D * D * N + 2 * 2 * (N // L) * L * L * D
 
@@ -27,6 +28,7 @@ def tile_scriptwriter_cpre_b_kernel(tc, base, x, wq, wk, wv, bv, w1, b1, w2, b2,
     with (
         tc.tile_pool(name="held", bufs=1) as held,
         tc.tile_pool(name="work", bufs=2) as work,
+        tc.tile_pool(name="norm_pool", bufs=SEQS) as norm_pool,
         tc.tile_pool(name="small", bufs=4) as small,
         tc.psum_pool(name="acc_pool", bufs=4) as acc_pool,
         tc.psum_pool(name="attn_pool", bufs=1) as attn_pool,
@@ -138,6 +140,9 @@ def tile_scriptwriter_cpre_b_kernel(tc, base, x, wq, wk, wv, bv, w1, b1, w2, b2,
             a_bf = work.tile([P, SEQS, L], BF16, name="a_bf")
             for s in range(SEQS):
                 nc.vector.tensor_scalar_mul(a_bf[:, s, :], e[:, s, :], inv_sums[:, s : s + 1])
+            return a_bf
+
+        def flip_weights(a_bf):
             at_ps = attn_pool.tile([P, SEQS, L], BF16, name="at_ps")
             for s in range(SEQS):
                 nc.tensor.transpose(at_ps[:, s, :], a_bf[:, s, :], ident_b[:])
@@ -152,7 +157,7 @@ def tile_scriptwriter_cpre_b_kernel(tc, base, x, wq, wk, wv, bv, w1, b1, w2, b2,
                 for s in range(SEQS):
                     nc.tensor.matmul(acc[:, block(s)], vt_sb[:, c * SEQS + s, block(b)], at_sb[:, s, :], start=True, stop=True)
                 nc.vector.tensor_tensor(y_sb[b][:, chunk], acc[:], x_sb[:, b, chunk], ADD)
-                nc.gpsimd.tensor_copy(y_bf[:, b, chunk], y_sb[b][:, chunk])
+                nc.scalar.copy(y_bf[:, b, chunk], y_sb[b][:, chunk])
 
         def feed_forward_hidden(c):
             chunk = slice(c * CHUNK, (c + 1) * CHUNK)
@@ -162,36 +167,51 @@ def tile_scriptwriter_cpre_b_kernel(tc, base, x, wq, wk, wv, bv, w1, b1, w2, b2,
                     nc.tensor.matmul(acc[:], w1_sb[:, kb, block(m)], y_bf[:, kb, chunk], start=(kb == 0), stop=(kb == DB - 1))
                 nc.scalar.activation(r_sb[:, m, chunk], acc[:], RELU, bias=b1_col[m])
 
-        def feed_forward_out_and_norm(c):
-            for u in range(c * SEQS, (c + 1) * SEQS):
-                acc = acc_pool.tile([P, D], F32, name="acc")
-                for eb in range(DB):
-                    nc.tensor.matmul(acc[:], r_sb[:, eb, block(u)], w2_sb[:, eb, :], start=(eb == 0), stop=(eb == DB - 1))
-                h = work.tile([P, D], F32, name="h")
-                nc.vector.tensor_tensor(h[:], acc[:], b2_all[:], ADD)
-                stats = small.tile([P, 6], F32, name="stats")
-                nc.vector.bn_stats(stats[:], h[:])
-                mean_var = small.tile([P, 2], F32, name="mean_var")
-                nc.vector.bn_aggr(mean_var[:], stats[:])
-                std = small.tile([P, 1], F32, name="std")
-                nc.scalar.activation(std[:], mean_var[:, 1:2], SQRT, bias=eps_col[:])
-                inv_std = small.tile([P, 1], F32, name="inv_std")
-                nc.vector.reciprocal(inv_std[:], std[:])
-                normed = work.tile([P, D], F32, name="normed")
-                nc.vector.tensor_scalar(normed[:], h[:], mean_var[:, 0:1], inv_std[:], SUB, MULT)
-                flipped = flip_pool.tile([P, DB, P], F32, name="flipped")
-                for b in range(DB):
-                    nc.tensor.transpose(flipped[:, b, :], normed[:, block(b)], ident_f[:])
-                for b in range(DB):
-                    nc.scalar.activation(z_sb[b][:, block(u)], flipped[:, b, :], IDENTITY, bias=shift_col[b], scale=gain_col[b])
+        def feed_forward_out_and_norm(u):
+            acc = acc_pool.tile([P, D], F32, name="acc")
+            for eb in range(DB):
+                nc.tensor.matmul(acc[:], r_sb[:, eb, block(u)], w2_sb[:, eb, :], start=(eb == 0), stop=(eb == DB - 1))
+            h = work.tile([P, D], F32, name="h")
+            nc.vector.tensor_tensor(h[:], acc[:], b2_all[:], ADD)
+            stats = small.tile([P, 6], F32, name="stats")
+            nc.vector.bn_stats(stats[:], h[:])
+            mean_var = small.tile([P, 2], F32, name="mean_var")
+            nc.vector.bn_aggr(mean_var[:], stats[:])
+            std = small.tile([P, 1], F32, name="std")
+            nc.scalar.activation(std[:], mean_var[:, 1:2], SQRT, bias=eps_col[:])
+            inv_std = small.tile([P, 1], F32, name="inv_std")
+            nc.vector.reciprocal(inv_std[:], std[:])
+            normed = norm_pool.tile([P, D], F32, name="normed")
+            nc.vector.tensor_scalar(normed[:], h[:], mean_var[:, 0:1], inv_std[:], SUB, MULT)
+            return normed
 
-        for c in range(N // CHUNK):
-            project_qk(c)
-            project_v(c)
-            at_sb = attention_weights(c)
-            attend(c, at_sb)
-            feed_forward_hidden(c)
-            feed_forward_out_and_norm(c)
+        def back_to_channels_first(u, normed):
+            flipped = flip_pool.tile([P, DB, P], F32, name="flipped")
+            for b in range(DB):
+                nc.tensor.transpose(flipped[:, b, :], normed[:, block(b)], ident_f[:])
+            for b in range(DB):
+                nc.scalar.activation(z_sb[b][:, block(u)], flipped[:, b, :], IDENTITY, bias=shift_col[b], scale=gain_col[b])
+
+        project_qk(0)
+        project_v(0)
+        a_bf0 = attention_weights(0)
+        project_qk(1)
+        attend(0, flip_weights(a_bf0))
+        project_v(1)
+        a_bf1 = attention_weights(1)
+        feed_forward_hidden(0)
+        attend(1, flip_weights(a_bf1))
+        normed_of = {}
+        for u in range(SEQS):
+            normed_of[u] = feed_forward_out_and_norm(u)
+        feed_forward_hidden(1)
+        for u in range(SEQS):
+            back_to_channels_first(u, normed_of[u])
+        for u in range(SEQS, 2 * SEQS + LAG):
+            if u < 2 * SEQS:
+                normed_of[u] = feed_forward_out_and_norm(u)
+            if u - LAG >= SEQS:
+                back_to_channels_first(u - LAG, normed_of[u - LAG])
 
         for b in range(DB):
             nc.vector.tensor_tensor(windows[b][:].indirect(offsets[:]), z_sb[b][:], y_sb[b][:], ADD)

@@ -11,7 +11,6 @@ L = 128
 DB = D // P
 CHUNK = 512
 SEQS = CHUNK // L
-LAG = 2
 EPS = 1e-8
 FLOPS = 2 * 5 * D * D * N + 2 * 2 * (N // L) * L * L * D
 
@@ -28,19 +27,16 @@ def tile_scriptwriter_cpre_b_kernel(tc, base, x, wq, wk, wv, bv, w1, b1, w2, b2,
     with (
         tc.tile_pool(name="held", bufs=1) as held,
         tc.tile_pool(name="work", bufs=2) as work,
-        tc.tile_pool(name="norm_pool", bufs=SEQS) as norm_pool,
         tc.tile_pool(name="small", bufs=4) as small,
         tc.psum_pool(name="acc_pool", bufs=4) as acc_pool,
         tc.psum_pool(name="attn_pool", bufs=1) as attn_pool,
         tc.psum_pool(name="flip_pool", bufs=2) as flip_pool,
     ):
-        offsets = held.tile([P, N // 16], U16, name="offsets")
-        nc.sync.dma_start(offsets[:], offs)
-
         x_sb = held.tile([P, DB, N], BF16, name="x_sb")
         x_blocks = x.rearrange("(kb p) n -> p kb n", p=P)
-        for kb in range(DB):
-            nc.sync.dma_start(x_sb[:, kb, :], x_blocks[:, kb, :])
+
+        def load_x(c):
+            nc.sync.dma_start(x_sb[:, :, c * CHUNK : (c + 1) * CHUNK], x_blocks[:, :, c * CHUNK : (c + 1) * CHUNK])
 
         def load_weight(w, name):
             w_sb = held.tile([P, DB, D], BF16, name=name)
@@ -52,10 +48,12 @@ def tile_scriptwriter_cpre_b_kernel(tc, base, x, wq, wk, wv, bv, w1, b1, w2, b2,
             nc.sync.dma_start(vec_all[:], vec.rearrange("d one -> (d one)").partition_broadcast(P))
             return vec_all
 
+        load_x(0)
         wq_sb = load_weight(wq, "wq_sb")
         wk_sb = load_weight(wk, "wk_sb")
         wv_sb = load_weight(wv, "wv_sb")
         bv_all = load_along_free_axis(bv, "bv_all")
+        load_x(1)
 
         rows = held.tile([P, P], F32, name="rows")
         nc.vector.memset(rows[:], 0.0)
@@ -66,6 +64,8 @@ def tile_scriptwriter_cpre_b_kernel(tc, base, x, wq, wk, wv, bv, w1, b1, w2, b2,
         w2_sb = load_weight(w2, "w2_sb")
         b2_all = load_along_free_axis(b2, "b2_all")
 
+        offsets = held.tile([P, N // 16], U16, name="offsets")
+        nc.sync.dma_start(offsets[:], offs)
         windows = [held.tile([P, S], F32, name=f"window{b}") for b in range(DB)]
         for b in range(DB):
             nc.sync.dma_start(windows[b][:], base[b * P : (b + 1) * P, :])
@@ -77,10 +77,13 @@ def tile_scriptwriter_cpre_b_kernel(tc, base, x, wq, wk, wv, bv, w1, b1, w2, b2,
         eps_col = held.tile([P, 1], F32, name="eps_col")
         nc.vector.memset(eps_col[:], EPS)
 
-        flipped = flip_pool.tile([P, DB, P], F32, name="flipped")
-        nc.tensor.transpose(flipped[:, 0, :], rows[:], ident_f[:])
         cols = held.tile([P, 3 * DB], F32, name="cols")
-        nc.vector.tensor_copy(cols[:], flipped[:, 0, 0 : 3 * DB])
+
+        def rows_to_cols():
+            flipped = flip_pool.tile([P, CHUNK], F32, name="flipped")
+            nc.tensor.transpose(flipped[:, 0:P], rows[:], ident_f[:])
+            nc.vector.tensor_copy(cols[:], flipped[:, 0 : 3 * DB])
+
         b1_col = [cols[:, b : b + 1] for b in range(DB)]
         gain_col = [cols[:, DB + b : DB + b + 1] for b in range(DB)]
         shift_col = [cols[:, 2 * DB + b : 2 * DB + b + 1] for b in range(DB)]
@@ -92,6 +95,7 @@ def tile_scriptwriter_cpre_b_kernel(tc, base, x, wq, wk, wv, bv, w1, b1, w2, b2,
         r_sb = held.tile([P, DB, N], BF16, name="r_sb")
         y_sb = [held.tile([P, N], F32, name=f"y{b}") for b in range(DB)]
         z_sb = [held.tile([P, N], F32, name=f"z{b}") for b in range(DB)]
+        normed = held.tile([P, N // L, D], F32, name="normed")
 
         def block(i):
             return slice(i * P, (i + 1) * P)
@@ -109,14 +113,13 @@ def tile_scriptwriter_cpre_b_kernel(tc, base, x, wq, wk, wv, bv, w1, b1, w2, b2,
                     nc.tensor.matmul(acc[:], wk_sb[:, kb, block(m)], x_sb[:, kb, chunk], start=(kb == 0), stop=(kb == DB - 1))
                 nc.vector.tensor_scalar_max(k_sb[:, m, chunk], acc[:], 0.0)
 
-        def project_v(c):
-            for u in range(c * SEQS, (c + 1) * SEQS):
-                acc = acc_pool.tile([P, D], F32, name="acc")
-                for kb in range(DB):
-                    nc.tensor.matmul(acc[:], x_sb[:, kb, block(u)], wv_sb[:, kb, :], start=(kb == 0), stop=(kb == DB - 1))
-                v_pre = work.tile([P, D], F32, name="v_pre")
-                nc.vector.tensor_tensor(v_pre[:], acc[:], bv_all[:], ADD)
-                nc.gpsimd.tensor_scalar_max(vt_sb[:, u, :], v_pre[:], 0.0)
+        def project_v(u):
+            acc = acc_pool.tile([P, D], F32, name="acc")
+            for kb in range(DB):
+                nc.tensor.matmul(acc[:], x_sb[:, kb, block(u)], wv_sb[:, kb, :], start=(kb == 0), stop=(kb == DB - 1))
+            v_pre = work.tile([P, D], F32, name="v_pre")
+            nc.vector.tensor_tensor(v_pre[:], acc[:], bv_all[:], ADD)
+            nc.gpsimd.tensor_scalar_max(vt_sb[:, u, :], v_pre[:], 0.0)
 
         def attention_weights(c):
             scores = attn_pool.tile([P, SEQS, L], F32, name="scores")
@@ -181,38 +184,40 @@ def tile_scriptwriter_cpre_b_kernel(tc, base, x, wq, wk, wv, bv, w1, b1, w2, b2,
             nc.scalar.activation(std[:], mean_var[:, 1:2], SQRT, bias=eps_col[:])
             inv_std = small.tile([P, 1], F32, name="inv_std")
             nc.vector.reciprocal(inv_std[:], std[:])
-            normed = norm_pool.tile([P, D], F32, name="normed")
-            nc.vector.tensor_scalar(normed[:], h[:], mean_var[:, 0:1], inv_std[:], SUB, MULT)
-            return normed
+            nc.vector.tensor_scalar(normed[:, u, :], h[:], mean_var[:, 0:1], inv_std[:], SUB, MULT)
 
-        def back_to_channels_first(u, normed):
-            flipped = flip_pool.tile([P, DB, P], F32, name="flipped")
-            for b in range(DB):
-                nc.tensor.transpose(flipped[:, b, :], normed[:, block(b)], ident_f[:])
-            for b in range(DB):
-                nc.scalar.activation(z_sb[b][:, block(u)], flipped[:, b, :], IDENTITY, bias=shift_col[b], scale=gain_col[b])
+        def back_to_channels_first(b):
+            for c in range(N // CHUNK):
+                flipped = flip_pool.tile([P, CHUNK], F32, name="flipped")
+                for s in range(SEQS):
+                    nc.tensor.transpose(flipped[:, block(s)], normed[:, c * SEQS + s, block(b)], ident_f[:])
+                nc.scalar.activation(
+                    z_sb[b][:, c * CHUNK : (c + 1) * CHUNK], flipped[:], IDENTITY, bias=shift_col[b], scale=gain_col[b]
+                )
 
         project_qk(0)
-        project_v(0)
+        rows_to_cols()
+        for u in range(SEQS):
+            project_v(u)
         a_bf0 = attention_weights(0)
         project_qk(1)
-        attend(0, flip_weights(a_bf0))
-        project_v(1)
+        at_sb0 = flip_weights(a_bf0)
+        project_v(SEQS)
+        attend(0, at_sb0)
+        for u in range(SEQS + 1, 2 * SEQS):
+            project_v(u)
         a_bf1 = attention_weights(1)
         feed_forward_hidden(0)
-        attend(1, flip_weights(a_bf1))
-        normed_of = {}
-        for u in range(SEQS):
-            normed_of[u] = feed_forward_out_and_norm(u)
+        at_sb1 = flip_weights(a_bf1)
+        feed_forward_out_and_norm(0)
+        attend(1, at_sb1)
+        for u in range(1, SEQS):
+            feed_forward_out_and_norm(u)
         feed_forward_hidden(1)
-        for u in range(SEQS):
-            back_to_channels_first(u, normed_of[u])
-        for u in range(SEQS, 2 * SEQS + LAG):
-            if u < 2 * SEQS:
-                normed_of[u] = feed_forward_out_and_norm(u)
-            if u - LAG >= SEQS:
-                back_to_channels_first(u - LAG, normed_of[u - LAG])
+        for u in range(SEQS, 2 * SEQS):
+            feed_forward_out_and_norm(u)
 
         for b in range(DB):
+            back_to_channels_first(b)
             nc.vector.tensor_tensor(windows[b][:].indirect(offsets[:]), z_sb[b][:], y_sb[b][:], ADD)
             nc.sync.dma_start(out[b * P : (b + 1) * P, :], windows[b][:])

@@ -18,6 +18,7 @@ BF16, F32, U16 = mybir.dt.bfloat16, mybir.dt.float32, mybir.dt.uint16
 ADD, SUB, MULT = mybir.AluOpType.add, mybir.AluOpType.subtract, mybir.AluOpType.mult
 RELU = mybir.ActivationFunctionType.Relu
 EXP = mybir.ActivationFunctionType.Exp
+SQUARE = mybir.ActivationFunctionType.Square
 SQRT = mybir.ActivationFunctionType.Sqrt
 IDENTITY = mybir.ActivationFunctionType.Identity
 
@@ -28,15 +29,18 @@ def tile_scriptwriter_cpre_b_kernel(tc, base, x, wq, wk, wv, bv, w1, b1, w2, b2,
         tc.tile_pool(name="held", bufs=1) as held,
         tc.tile_pool(name="work", bufs=2) as work,
         tc.tile_pool(name="small", bufs=4) as small,
-        tc.psum_pool(name="acc_pool", bufs=4) as acc_pool,
+        tc.psum_pool(name="acc_pool", bufs=5) as acc_pool,
         tc.psum_pool(name="attn_pool", bufs=1) as attn_pool,
         tc.psum_pool(name="flip_pool", bufs=2) as flip_pool,
     ):
-        x_sb = held.tile([P, DB, N], BF16, name="x_sb")
-        x_blocks = x.rearrange("(kb p) n -> p kb n", p=P)
+        def block(i):
+            return slice(i * P, (i + 1) * P)
 
-        def load_x(c):
-            nc.sync.dma_start(x_sb[:, :, c * CHUNK : (c + 1) * CHUNK], x_blocks[:, :, c * CHUNK : (c + 1) * CHUNK])
+        x_sb = held.tile([P, DB, N], BF16, name="x_sb")
+        wq_sb = held.tile([P, DB, D], BF16, name="wq_sb")
+        for kb in range(DB):
+            nc.sync.dma_start(x_sb[:, kb, 0:CHUNK], x[block(kb), 0:CHUNK])
+            nc.sync.dma_start(wq_sb[:, kb, :], wq[block(kb), :])
 
         def load_weight(w, name):
             w_sb = held.tile([P, DB, D], BF16, name=name)
@@ -48,12 +52,10 @@ def tile_scriptwriter_cpre_b_kernel(tc, base, x, wq, wk, wv, bv, w1, b1, w2, b2,
             nc.sync.dma_start(vec_all[:], vec.rearrange("d one -> (d one)").partition_broadcast(P))
             return vec_all
 
-        load_x(0)
-        wq_sb = load_weight(wq, "wq_sb")
         wk_sb = load_weight(wk, "wk_sb")
         wv_sb = load_weight(wv, "wv_sb")
         bv_all = load_along_free_axis(bv, "bv_all")
-        load_x(1)
+        nc.sync.dma_start(x_sb[:, :, CHUNK:N], x.rearrange("(kb p) n -> p kb n", p=P)[:, :, CHUNK:N])
 
         rows = held.tile([P, P], F32, name="rows")
         nc.vector.memset(rows[:], 0.0)
@@ -95,18 +97,21 @@ def tile_scriptwriter_cpre_b_kernel(tc, base, x, wq, wk, wv, bv, w1, b1, w2, b2,
         r_sb = held.tile([P, DB, N], BF16, name="r_sb")
         y_sb = [held.tile([P, N], F32, name=f"y{b}") for b in range(DB)]
         z_sb = [held.tile([P, N], F32, name=f"z{b}") for b in range(DB)]
-        normed = held.tile([P, N // L, D], F32, name="normed")
-
-        def block(i):
-            return slice(i * P, (i + 1) * P)
+        h_sb = held.tile([P, N // L, D], F32, name="h_sb")
+        sum_h = held.tile([P, N // L], F32, name="sum_h")
+        neg_mean = held.tile([P, N // L], F32, name="neg_mean")
+        sum_sq = held.tile([P, N // L], F32, name="sum_sq")
+        inv_std = held.tile([P, N // L], F32, name="inv_std")
+        neg_mean_scaled = held.tile([P, N // L], F32, name="neg_mean_scaled")
 
         def project_qk(c):
             chunk = slice(c * CHUNK, (c + 1) * CHUNK)
+            accs = [acc_pool.tile([P, CHUNK], F32, name="acc") for m in range(DB)]
+            for kb in range(DB):
+                for m in range(DB):
+                    nc.tensor.matmul(accs[m][:], wq_sb[:, kb, block(m)], x_sb[:, kb, chunk], start=(kb == 0), stop=(kb == DB - 1))
             for m in range(DB):
-                acc = acc_pool.tile([P, CHUNK], F32, name="acc")
-                for kb in range(DB):
-                    nc.tensor.matmul(acc[:], wq_sb[:, kb, block(m)], x_sb[:, kb, chunk], start=(kb == 0), stop=(kb == DB - 1))
-                nc.scalar.activation(q_sb[:, m, chunk], acc[:], RELU)
+                nc.scalar.activation(q_sb[:, m, chunk], accs[m][:], RELU)
             for m in range(DB):
                 acc = acc_pool.tile([P, CHUNK], F32, name="acc")
                 for kb in range(DB):
@@ -122,7 +127,7 @@ def tile_scriptwriter_cpre_b_kernel(tc, base, x, wq, wk, wv, bv, w1, b1, w2, b2,
             nc.gpsimd.tensor_scalar_max(vt_sb[:, u, :], v_pre[:], 0.0)
 
         def attention_weights(c):
-            scores = attn_pool.tile([P, SEQS, L], F32, name="scores")
+            scores = attn_pool.tile([P, SEQS, L], F32, name="scores", tag="attn")
             for s in range(SEQS):
                 u = c * SEQS + s
                 for m in range(DB):
@@ -146,7 +151,7 @@ def tile_scriptwriter_cpre_b_kernel(tc, base, x, wq, wk, wv, bv, w1, b1, w2, b2,
             return a_bf
 
         def flip_weights(a_bf):
-            at_ps = attn_pool.tile([P, SEQS, L], BF16, name="at_ps")
+            at_ps = attn_pool.tile([P, SEQS, L], BF16, name="at_ps", tag="attn")
             for s in range(SEQS):
                 nc.tensor.transpose(at_ps[:, s, :], a_bf[:, s, :], ident_b[:])
             at_sb = work.tile([P, SEQS, L], BF16, name="at_sb")
@@ -170,30 +175,40 @@ def tile_scriptwriter_cpre_b_kernel(tc, base, x, wq, wk, wv, bv, w1, b1, w2, b2,
                     nc.tensor.matmul(acc[:], w1_sb[:, kb, block(m)], y_bf[:, kb, chunk], start=(kb == 0), stop=(kb == DB - 1))
                 nc.scalar.activation(r_sb[:, m, chunk], acc[:], RELU, bias=b1_col[m])
 
-        def feed_forward_out_and_norm(u):
+        def feed_forward_out(u):
             acc = acc_pool.tile([P, D], F32, name="acc")
             for eb in range(DB):
                 nc.tensor.matmul(acc[:], r_sb[:, eb, block(u)], w2_sb[:, eb, :], start=(eb == 0), stop=(eb == DB - 1))
-            h = work.tile([P, D], F32, name="h")
-            nc.vector.tensor_tensor(h[:], acc[:], b2_all[:], ADD)
-            stats = small.tile([P, 6], F32, name="stats")
-            nc.vector.bn_stats(stats[:], h[:])
-            mean_var = small.tile([P, 2], F32, name="mean_var")
-            nc.vector.bn_aggr(mean_var[:], stats[:])
-            std = small.tile([P, 1], F32, name="std")
-            nc.scalar.activation(std[:], mean_var[:, 1:2], SQRT, bias=eps_col[:])
-            inv_std = small.tile([P, 1], F32, name="inv_std")
-            nc.vector.reciprocal(inv_std[:], std[:])
-            nc.vector.tensor_scalar(normed[:, u, :], h[:], mean_var[:, 0:1], inv_std[:], SUB, MULT)
+            one = slice(u, u + 1)
+            nc.vector.scalar_tensor_tensor(h_sb[:, u, :], acc[:], 1.0, b2_all[:], MULT, ADD, accum_out=sum_h[:, one])
+            nc.vector.tensor_scalar_mul(neg_mean[:, one], sum_h[:, one], -1.0 / D)
+            squares = work.tile([P, D], F32, name="squares")
+            nc.scalar.activation(squares[:], h_sb[:, u, :], SQUARE, bias=neg_mean[:, one], accum_out=sum_sq[:, one])
 
-        def back_to_channels_first(b):
-            for c in range(N // CHUNK):
-                flipped = flip_pool.tile([P, CHUNK], F32, name="flipped")
-                for s in range(SEQS):
-                    nc.tensor.transpose(flipped[:, block(s)], normed[:, c * SEQS + s, block(b)], ident_f[:])
+        def inverse_std(c):
+            blocks = slice(c * SEQS, (c + 1) * SEQS)
+            std = small.tile([P, SEQS], F32, name="std")
+            nc.scalar.activation(std[:], sum_sq[:, blocks], SQRT, bias=eps_col[:], scale=1.0 / D)
+            nc.vector.reciprocal(inv_std[:, blocks], std[:])
+            nc.vector.tensor_tensor(neg_mean_scaled[:, blocks], neg_mean[:, blocks], inv_std[:, blocks], MULT)
+
+        def make_z(b, c):
+            normed = work.tile([P, SEQS, P], F32, name="normed")
+            flipped = flip_pool.tile([P, CHUNK], F32, name="flipped")
+            for s in range(SEQS):
+                u = c * SEQS + s
                 nc.scalar.activation(
-                    z_sb[b][:, c * CHUNK : (c + 1) * CHUNK], flipped[:], IDENTITY, bias=shift_col[b], scale=gain_col[b]
+                    normed[:, s, :], h_sb[:, u, block(b)], IDENTITY,
+                    bias=neg_mean_scaled[:, u : u + 1], scale=inv_std[:, u : u + 1],
                 )
+                nc.tensor.transpose(flipped[:, block(s)], normed[:, s, :], ident_f[:])
+            nc.scalar.activation(
+                z_sb[b][:, c * CHUNK : (c + 1) * CHUNK], flipped[:], IDENTITY, bias=shift_col[b], scale=gain_col[b]
+            )
+
+        def place(b):
+            nc.vector.tensor_tensor(windows[b][:].indirect(offsets[:]), z_sb[b][:], y_sb[b][:], ADD)
+            nc.sync.dma_start(out[b * P : (b + 1) * P, :], windows[b][:])
 
         project_qk(0)
         rows_to_cols()
@@ -209,15 +224,19 @@ def tile_scriptwriter_cpre_b_kernel(tc, base, x, wq, wk, wv, bv, w1, b1, w2, b2,
         a_bf1 = attention_weights(1)
         feed_forward_hidden(0)
         at_sb1 = flip_weights(a_bf1)
-        feed_forward_out_and_norm(0)
+        feed_forward_out(0)
         attend(1, at_sb1)
         for u in range(1, SEQS):
-            feed_forward_out_and_norm(u)
+            feed_forward_out(u)
+        inverse_std(0)
         feed_forward_hidden(1)
         for u in range(SEQS, 2 * SEQS):
-            feed_forward_out_and_norm(u)
-
-        for b in range(DB):
-            back_to_channels_first(b)
-            nc.vector.tensor_tensor(windows[b][:].indirect(offsets[:]), z_sb[b][:], y_sb[b][:], ADD)
-            nc.sync.dma_start(out[b * P : (b + 1) * P, :], windows[b][:])
+            feed_forward_out(u)
+        make_z(0, 0)
+        inverse_std(1)
+        make_z(0, 1)
+        place(0)
+        for b in range(1, DB):
+            make_z(b, 0)
+            make_z(b, 1)
+            place(b)

@@ -122,9 +122,9 @@ def tile_scriptwriter_cpre_b_kernel(tc, base, x, wq, wk, wv, bv, w1, b1, w2, b2,
             acc = acc_pool.tile([P, D], F32, name="acc")
             for kb in range(DB):
                 nc.tensor.matmul(acc[:], x_sb[:, kb, block(u)], wv_sb[:, kb, :], start=(kb == 0), stop=(kb == DB - 1))
-            v_pre = work.tile([P, D], F32, name="v_pre")
+            v_pre = work.tile([P, D], BF16, name="v_pre")
             nc.vector.tensor_tensor(v_pre[:], acc[:], bv_all[:], ADD)
-            nc.gpsimd.tensor_scalar_max(vt_sb[:, u, :], v_pre[:], 0.0)
+            nc.vector.tensor_scalar_max(vt_sb[:, u, :], v_pre[:], 0.0)
 
         def attention_weights(c):
             scores = attn_pool.tile([P, SEQS, L], F32, name="scores", tag="attn")
@@ -185,12 +185,19 @@ def tile_scriptwriter_cpre_b_kernel(tc, base, x, wq, wk, wv, bv, w1, b1, w2, b2,
             squares = work.tile([P, D], F32, name="squares")
             nc.scalar.activation(squares[:], h_sb[:, u, :], SQUARE, bias=neg_mean[:, one], accum_out=sum_sq[:, one])
 
-        def inverse_std(c):
-            blocks = slice(c * SEQS, (c + 1) * SEQS)
-            std = small.tile([P, SEQS], F32, name="std")
-            nc.scalar.activation(std[:], sum_sq[:, blocks], SQRT, bias=eps_col[:], scale=1.0 / D)
-            nc.vector.reciprocal(inv_std[:, blocks], std[:])
-            nc.vector.tensor_tensor(neg_mean_scaled[:, blocks], neg_mean[:, blocks], inv_std[:, blocks], MULT)
+        def inverse_std(u):
+            one = slice(u, u + 1)
+            std = small.tile([P, 1], F32, name="std")
+            nc.scalar.activation(std[:], sum_sq[:, one], SQRT, bias=eps_col[:], scale=1.0 / D)
+            nc.vector.reciprocal(inv_std[:, one], std[:])
+
+        def make_first_z(u):
+            one = slice(u, u + 1)
+            normed = work.tile([P, P], F32, name="normed_first")
+            nc.vector.tensor_scalar(normed[:], h_sb[:, u, block(0)], neg_mean[:, one], inv_std[:, one], ADD, MULT)
+            flipped = flip_pool.tile([P, P], F32, name="flipped")
+            nc.tensor.transpose(flipped[:], normed[:], ident_f[:])
+            nc.vector.tensor_scalar(z_sb[0][:, block(u)], flipped[:], gain_col[0], shift_col[0], MULT, ADD)
 
         def make_z(b, c):
             normed = work.tile([P, SEQS, P], F32, name="normed")
@@ -228,13 +235,19 @@ def tile_scriptwriter_cpre_b_kernel(tc, base, x, wq, wk, wv, bv, w1, b1, w2, b2,
         attend(1, at_sb1)
         for u in range(1, SEQS):
             feed_forward_out(u)
-        inverse_std(0)
+            inverse_std(u - 1)
+            make_first_z(u - 1)
+        inverse_std(SEQS - 1)
+        make_first_z(SEQS - 1)
         feed_forward_hidden(1)
-        for u in range(SEQS, 2 * SEQS):
+        feed_forward_out(SEQS)
+        for u in range(SEQS + 1, 2 * SEQS):
             feed_forward_out(u)
-        make_z(0, 0)
-        inverse_std(1)
-        make_z(0, 1)
+            inverse_std(u - 1)
+            make_first_z(u - 1)
+        inverse_std(2 * SEQS - 1)
+        make_first_z(2 * SEQS - 1)
+        nc.vector.tensor_tensor(neg_mean_scaled[:], neg_mean[:], inv_std[:], MULT)
         place(0)
         for b in range(1, DB):
             make_z(b, 0)

@@ -19,7 +19,7 @@ ADD, SUB, MULT = mybir.AluOpType.add, mybir.AluOpType.subtract, mybir.AluOpType.
 RELU = mybir.ActivationFunctionType.Relu
 EXP = mybir.ActivationFunctionType.Exp
 SQUARE = mybir.ActivationFunctionType.Square
-SQRT = mybir.ActivationFunctionType.Sqrt
+INV_SQRT = mybir.ActivationFunctionType.Abs_reciprocal_sqrt
 IDENTITY = mybir.ActivationFunctionType.Identity
 
 
@@ -181,15 +181,15 @@ def tile_scriptwriter_cpre_b_kernel(tc, base, x, wq, wk, wv, bv, w1, b1, w2, b2,
                 nc.tensor.matmul(acc[:], r_sb[:, eb, block(u)], w2_sb[:, eb, :], start=(eb == 0), stop=(eb == DB - 1))
             one = slice(u, u + 1)
             nc.vector.scalar_tensor_tensor(h_sb[:, u, :], acc[:], 1.0, b2_all[:], MULT, ADD, accum_out=sum_h[:, one])
-            nc.vector.tensor_scalar_mul(neg_mean[:, one], sum_h[:, one], -1.0 / D)
             squares = work.tile([P, D], F32, name="squares")
-            nc.scalar.activation(squares[:], h_sb[:, u, :], SQUARE, bias=neg_mean[:, one], accum_out=sum_sq[:, one])
+            nc.scalar.activation(
+                squares[:], h_sb[:, u, :], SQUARE, bias=sum_h[:, one], scale=-float(D), accum_out=sum_sq[:, one]
+            )
+            nc.vector.tensor_scalar_mul(neg_mean[:, one], sum_h[:, one], -1.0 / D)
 
         def inverse_std(u):
             one = slice(u, u + 1)
-            std = small.tile([P, 1], F32, name="std")
-            nc.scalar.activation(std[:], sum_sq[:, one], SQRT, bias=eps_col[:], scale=1.0 / D)
-            nc.vector.reciprocal(inv_std[:, one], std[:])
+            nc.scalar.activation(inv_std[:, one], sum_sq[:, one], INV_SQRT, bias=eps_col[:], scale=1.0 / D**3)
 
         def make_first_z(u):
             one = slice(u, u + 1)

@@ -104,7 +104,7 @@ def tile_scriptwriter_cpre_b_kernel(tc, base, x, wq, wk, wv, bv, w1, b1, w2, b2,
         inv_std = held.tile([P, N // L], F32, name="inv_std")
         neg_mean_scaled = held.tile([P, N // L], F32, name="neg_mean_scaled")
 
-        def project_qk(c):
+        def project_q(c):
             chunk = slice(c * CHUNK, (c + 1) * CHUNK)
             accs = [acc_pool.tile([P, CHUNK], F32, name="acc") for m in range(DB)]
             for kb in range(DB):
@@ -112,6 +112,9 @@ def tile_scriptwriter_cpre_b_kernel(tc, base, x, wq, wk, wv, bv, w1, b1, w2, b2,
                     nc.tensor.matmul(accs[m][:], wq_sb[:, kb, block(m)], x_sb[:, kb, chunk], start=(kb == 0), stop=(kb == DB - 1))
             for m in range(DB):
                 nc.scalar.activation(q_sb[:, m, chunk], accs[m][:], RELU)
+
+        def project_k(c):
+            chunk = slice(c * CHUNK, (c + 1) * CHUNK)
             for m in range(DB):
                 acc = acc_pool.tile([P, CHUNK], F32, name="acc")
                 for kb in range(DB):
@@ -217,36 +220,35 @@ def tile_scriptwriter_cpre_b_kernel(tc, base, x, wq, wk, wv, bv, w1, b1, w2, b2,
             nc.vector.tensor_tensor(windows[b][:].indirect(offsets[:]), z_sb[b][:], y_sb[b][:], ADD)
             nc.sync.dma_start(out[b * P : (b + 1) * P, :], windows[b][:])
 
-        project_qk(0)
+        def feed_forward_out_and_first_z(c):
+            blocks = range(c * SEQS, (c + 1) * SEQS)
+            for u in blocks:
+                feed_forward_out(u)
+                if u > blocks[0]:
+                    inverse_std(u - 1)
+                    make_first_z(u - 1)
+            inverse_std(blocks[-1])
+            make_first_z(blocks[-1])
+
+        project_q(0)
+        project_k(0)
         rows_to_cols()
         for u in range(SEQS):
             project_v(u)
         a_bf0 = attention_weights(0)
-        project_qk(1)
+        project_q(1)
         at_sb0 = flip_weights(a_bf0)
-        project_v(SEQS)
+        project_k(1)
         attend(0, at_sb0)
-        for u in range(SEQS + 1, 2 * SEQS):
-            project_v(u)
         a_bf1 = attention_weights(1)
-        feed_forward_hidden(0)
+        for u in range(SEQS, 2 * SEQS):
+            project_v(u)
         at_sb1 = flip_weights(a_bf1)
-        feed_forward_out(0)
+        feed_forward_hidden(0)
         attend(1, at_sb1)
-        for u in range(1, SEQS):
-            feed_forward_out(u)
-            inverse_std(u - 1)
-            make_first_z(u - 1)
-        inverse_std(SEQS - 1)
-        make_first_z(SEQS - 1)
+        feed_forward_out_and_first_z(0)
         feed_forward_hidden(1)
-        feed_forward_out(SEQS)
-        for u in range(SEQS + 1, 2 * SEQS):
-            feed_forward_out(u)
-            inverse_std(u - 1)
-            make_first_z(u - 1)
-        inverse_std(2 * SEQS - 1)
-        make_first_z(2 * SEQS - 1)
+        feed_forward_out_and_first_z(1)
         nc.vector.tensor_tensor(neg_mean_scaled[:], neg_mean[:], inv_std[:], MULT)
         place(0)
         for b in range(1, DB):

@@ -194,13 +194,18 @@ def tile_scriptwriter_cpre_b_kernel(tc, base, x, wq, wk, wv, bv, w1, b1, w2, b2,
             one = slice(u, u + 1)
             nc.scalar.activation(inv_std[:, one], sum_sq[:, one], INV_SQRT, bias=eps_col[:], scale=1.0 / D**3)
 
-        def make_first_z(u):
-            one = slice(u, u + 1)
-            normed = work.tile([P, P], F32, name="normed_first")
-            nc.vector.tensor_scalar(normed[:], h_sb[:, u, block(0)], neg_mean[:, one], inv_std[:, one], ADD, MULT)
-            flipped = flip_pool.tile([P, P], F32, name="flipped")
-            nc.tensor.transpose(flipped[:], normed[:], ident_f[:])
-            nc.vector.tensor_scalar(z_sb[0][:, block(u)], flipped[:], gain_col[0], shift_col[0], MULT, ADD)
+        def make_first_z(first, count):
+            normed = work.tile([P, SEQS, P], F32, name="normed_first")
+            flipped = flip_pool.tile([P, CHUNK], F32, name="flipped")
+            for i in range(count):
+                u = first + i
+                nc.vector.tensor_scalar(
+                    normed[:, i, :], h_sb[:, u, block(0)], neg_mean[:, u : u + 1], inv_std[:, u : u + 1], ADD, MULT
+                )
+                nc.tensor.transpose(flipped[:, block(i)], normed[:, i, :], ident_f[:])
+            nc.vector.tensor_scalar(
+                z_sb[0][:, first * P : (first + count) * P], flipped[:, 0 : count * P], gain_col[0], shift_col[0], MULT, ADD
+            )
 
         def make_z(b, c):
             normed = work.tile([P, SEQS, P], F32, name="normed")
@@ -220,16 +225,6 @@ def tile_scriptwriter_cpre_b_kernel(tc, base, x, wq, wk, wv, bv, w1, b1, w2, b2,
             nc.vector.tensor_tensor(windows[b][:].indirect(offsets[:]), z_sb[b][:], y_sb[b][:], ADD)
             nc.sync.dma_start(out[b * P : (b + 1) * P, :], windows[b][:])
 
-        def feed_forward_out_and_first_z(c):
-            blocks = range(c * SEQS, (c + 1) * SEQS)
-            for u in blocks:
-                feed_forward_out(u)
-                if u > blocks[0]:
-                    inverse_std(u - 1)
-                    make_first_z(u - 1)
-            inverse_std(blocks[-1])
-            make_first_z(blocks[-1])
-
         project_q(0)
         project_k(0)
         rows_to_cols()
@@ -246,9 +241,16 @@ def tile_scriptwriter_cpre_b_kernel(tc, base, x, wq, wk, wv, bv, w1, b1, w2, b2,
         at_sb1 = flip_weights(a_bf1)
         feed_forward_hidden(0)
         attend(1, at_sb1)
-        feed_forward_out_and_first_z(0)
+        for u in range(SEQS):
+            feed_forward_out(u)
+            inverse_std(u)
         feed_forward_hidden(1)
-        feed_forward_out_and_first_z(1)
+        make_first_z(0, SEQS)
+        for u in range(SEQS, 2 * SEQS):
+            feed_forward_out(u)
+            inverse_std(u)
+        make_first_z(SEQS, SEQS // 2)
+        make_first_z(SEQS + SEQS // 2, SEQS // 2)
         nc.vector.tensor_tensor(neg_mean_scaled[:], neg_mean[:], inv_std[:], MULT)
         place(0)
         for b in range(1, DB):

@@ -190,22 +190,53 @@ def tile_scriptwriter_cpre_b_kernel(tc, base, x, wq, wk, wv, bv, w1, b1, w2, b2,
             )
             nc.vector.tensor_scalar_mul(neg_mean[:, one], sum_h[:, one], -1.0 / D)
 
+        def feed_forward_out_last(u):
+            half = D // 2
+            half_sum = small.tile([P, 2], F32, name="half_sum")
+            for i in range(2):
+                part = slice(i * half, (i + 1) * half)
+                acc = acc_pool.tile([P, CHUNK], F32, name="acc")
+                for eb in range(DB):
+                    nc.tensor.matmul(
+                        acc[:, 0:half], r_sb[:, eb, block(u)], w2_sb[:, eb, part], start=(eb == 0), stop=(eb == DB - 1)
+                    )
+                nc.vector.scalar_tensor_tensor(
+                    h_sb[:, u, part], acc[:, 0:half], 1.0, b2_all[:, part], MULT, ADD, accum_out=half_sum[:, i : i + 1]
+                )
+            one = slice(u, u + 1)
+            squares = work.tile([P, D], F32, name="squares")
+            nc.scalar.activation(
+                squares[:], h_sb[:, u, :], SQUARE, bias=half_sum[:, 0:1], scale=-float(half), accum_out=sum_sq[:, one]
+            )
+            mean_gap = small.tile([P, 1], F32, name="mean_gap")
+            nc.vector.tensor_scalar(mean_gap[:], half_sum[:, 1:2], half_sum[:, 0:1], 1.0 / D, SUB, MULT)
+            gap_sq = small.tile([P, 1], F32, name="gap_sq")
+            nc.vector.scalar_tensor_tensor(gap_sq[:], mean_gap[:], mean_gap[:], eps_col[:], MULT, SUB)
+            nc.vector.tensor_scalar(neg_mean[:, one], half_sum[:, 0:1], half_sum[:, 1:2], -1.0 / D, ADD, MULT)
+            return gap_sq
+
+        def inverse_std_last(u, gap_sq):
+            one = slice(u, u + 1)
+            nc.scalar.activation(
+                inv_std[:, one], sum_sq[:, one], INV_SQRT, bias=gap_sq[:], scale=-1.0 / ((D // 2) ** 2 * D)
+            )
+
         def inverse_std(u):
             one = slice(u, u + 1)
             nc.scalar.activation(inv_std[:, one], sum_sq[:, one], INV_SQRT, bias=eps_col[:], scale=1.0 / D**3)
 
-        def make_first_z(first, count):
+        def make_first_z(first, count, flipped):
             normed = work.tile([P, SEQS, P], F32, name="normed_first")
-            flipped = flip_pool.tile([P, CHUNK], F32, name="flipped")
             for i in range(count):
                 u = first + i
                 nc.vector.tensor_scalar(
                     normed[:, i, :], h_sb[:, u, block(0)], neg_mean[:, u : u + 1], inv_std[:, u : u + 1], ADD, MULT
                 )
                 nc.tensor.transpose(flipped[:, block(i)], normed[:, i, :], ident_f[:])
-            nc.vector.tensor_scalar(
-                z_sb[0][:, first * P : (first + count) * P], flipped[:, 0 : count * P], gain_col[0], shift_col[0], MULT, ADD
-            )
+            for i in range(count):
+                nc.vector.tensor_scalar(
+                    z_sb[0][:, block(first + i)], flipped[:, block(i)], gain_col[0], shift_col[0], MULT, ADD
+                )
 
         def make_z(b, c):
             normed = work.tile([P, SEQS, P], F32, name="normed")
@@ -245,12 +276,18 @@ def tile_scriptwriter_cpre_b_kernel(tc, base, x, wq, wk, wv, bv, w1, b1, w2, b2,
             feed_forward_out(u)
             inverse_std(u)
         feed_forward_hidden(1)
-        make_first_z(0, SEQS)
-        for u in range(SEQS, 2 * SEQS):
+        last = N // L - 1
+        for u in range(SEQS, last):
             feed_forward_out(u)
-            inverse_std(u)
-        make_first_z(SEQS, SEQS // 2)
-        make_first_z(SEQS + SEQS // 2, SEQS // 2)
+            if u < last - 1:
+                inverse_std(u)
+        gap_sq = feed_forward_out_last(last)
+        inverse_std(last - 1)
+        inverse_std_last(last, gap_sq)
+        make_first_z(0, SEQS, attn_pool.tile([P, CHUNK], F32, name="flipped_first", tag="attn"))
+        make_first_z(SEQS, SEQS - 2, flip_pool.tile([P, CHUNK], F32, name="flipped"))
+        make_first_z(last - 1, 1, flip_pool.tile([P, CHUNK], F32, name="flipped"))
+        make_first_z(last, 1, flip_pool.tile([P, CHUNK], F32, name="flipped"))
         nc.vector.tensor_tensor(neg_mean_scaled[:], neg_mean[:], inv_std[:], MULT)
         place(0)
         for b in range(1, DB):

@@ -192,27 +192,32 @@ def tile_scriptwriter_cpre_b_kernel(tc, base, x, wq, wk, wv, bv, w1, b1, w2, b2,
 
         def feed_forward_out_last(u):
             half = D // 2
-            half_sum = small.tile([P, 2], F32, name="half_sum")
-            for i in range(2):
-                part = slice(i * half, (i + 1) * half)
+            part_sum = small.tile([P, 3], F32, name="part_sum")
+            for i, (first, width) in enumerate(((0, half), (half, P), (half + P, P))):
+                part = slice(first, first + width)
                 acc = acc_pool.tile([P, CHUNK], F32, name="acc")
                 for eb in range(DB):
                     nc.tensor.matmul(
-                        acc[:, 0:half], r_sb[:, eb, block(u)], w2_sb[:, eb, part], start=(eb == 0), stop=(eb == DB - 1)
+                        acc[:, 0:width], r_sb[:, eb, block(u)], w2_sb[:, eb, part], start=(eb == 0), stop=(eb == DB - 1)
                     )
                 nc.vector.scalar_tensor_tensor(
-                    h_sb[:, u, part], acc[:, 0:half], 1.0, b2_all[:, part], MULT, ADD, accum_out=half_sum[:, i : i + 1]
+                    h_sb[:, u, part], acc[:, 0:width], 1.0, b2_all[:, part], MULT, ADD, accum_out=part_sum[:, i : i + 1]
                 )
+            sum_0, sum_1, sum_2 = (part_sum[:, i : i + 1] for i in range(3))
+            diff_01 = small.tile([P, 1], F32, name="diff_01")
+            nc.vector.tensor_tensor(diff_01[:], sum_0, sum_1, SUB)
+            sum_01 = small.tile([P, 1], F32, name="sum_01")
+            nc.vector.tensor_tensor(sum_01[:], sum_0, sum_1, ADD)
             one = slice(u, u + 1)
             squares = work.tile([P, D], F32, name="squares")
             nc.scalar.activation(
-                squares[:], h_sb[:, u, :], SQUARE, bias=half_sum[:, 0:1], scale=-float(half), accum_out=sum_sq[:, one]
+                squares[:], h_sb[:, u, :], SQUARE, bias=sum_0, scale=-float(half), accum_out=sum_sq[:, one]
             )
             mean_gap = small.tile([P, 1], F32, name="mean_gap")
-            nc.vector.tensor_scalar(mean_gap[:], half_sum[:, 1:2], half_sum[:, 0:1], 1.0 / D, SUB, MULT)
+            nc.vector.tensor_scalar(mean_gap[:], sum_2, diff_01[:], 1.0 / D, SUB, MULT)
             gap_sq = small.tile([P, 1], F32, name="gap_sq")
             nc.vector.scalar_tensor_tensor(gap_sq[:], mean_gap[:], mean_gap[:], eps_col[:], MULT, SUB)
-            nc.vector.tensor_scalar(neg_mean[:, one], half_sum[:, 0:1], half_sum[:, 1:2], -1.0 / D, ADD, MULT)
+            nc.vector.tensor_scalar(neg_mean[:, one], sum_2, sum_01[:], -1.0 / D, ADD, MULT)
             return gap_sq
 
         def inverse_std_last(u, gap_sq):

@@ -119,7 +119,10 @@ def tile_scriptwriter_cpre_b_kernel(tc, base, x, wq, wk, wv, bv, w1, b1, w2, b2,
                 acc = acc_pool.tile([P, CHUNK], F32, name="acc")
                 for kb in range(DB):
                     nc.tensor.matmul(acc[:], wk_sb[:, kb, block(m)], x_sb[:, kb, chunk], start=(kb == 0), stop=(kb == DB - 1))
-                nc.vector.tensor_scalar_max(k_sb[:, m, chunk], acc[:], 0.0)
+                if m % 2 == 0:
+                    nc.scalar.activation(k_sb[:, m, chunk], acc[:], RELU)
+                else:
+                    nc.vector.tensor_scalar_max(k_sb[:, m, chunk], acc[:], 0.0)
 
         def project_v(u):
             acc = acc_pool.tile([P, D], F32, name="acc")
@@ -277,10 +280,12 @@ def tile_scriptwriter_cpre_b_kernel(tc, base, x, wq, wk, wv, bv, w1, b1, w2, b2,
         at_sb1 = flip_weights(a_bf1)
         feed_forward_hidden(0)
         attend(1, at_sb1)
-        for u in range(SEQS):
+        for u in range(SEQS - 1):
             feed_forward_out(u)
             inverse_std(u)
         feed_forward_hidden(1)
+        feed_forward_out(SEQS - 1)
+        inverse_std(SEQS - 1)
         last = N // L - 1
         for u in range(SEQS, last):
             feed_forward_out(u)

import math

import concourse.mybir as mybir
from concourse.masks import make_identity

P = 128
D = 512
S = 4096
N = 1024
L = 128
DB = D // P
CHUNK = 512
SEQS = CHUNK // L
EPS = 1e-8
FLOPS = 2 * 5 * D * D * N + 2 * 2 * (N // L) * L * L * D

BF16, F32, U16 = mybir.dt.bfloat16, mybir.dt.float32, mybir.dt.uint16
ADD, SUB, MULT = mybir.AluOpType.add, mybir.AluOpType.subtract, mybir.AluOpType.mult
RELU = mybir.ActivationFunctionType.Relu
EXP = mybir.ActivationFunctionType.Exp
SQUARE = mybir.ActivationFunctionType.Square
INV_SQRT = mybir.ActivationFunctionType.Abs_reciprocal_sqrt
IDENTITY = mybir.ActivationFunctionType.Identity


def tile_scriptwriter_cpre_b_kernel(tc, base, x, wq, wk, wv, bv, w1, b1, w2, b2, gain, shift, offs, out):
    nc = tc.nc
    with (
        tc.tile_pool(name="held", bufs=1) as held,
        tc.tile_pool(name="work", bufs=2) as work,
        tc.tile_pool(name="small", bufs=4) as small,
        tc.psum_pool(name="acc_pool", bufs=5) as acc_pool,
        tc.psum_pool(name="attn_pool", bufs=1) as attn_pool,
        tc.psum_pool(name="flip_pool", bufs=2) as flip_pool,
    ):
        def block(i):
            return slice(i * P, (i + 1) * P)

        x_sb = held.tile([P, DB, N], BF16, name="x_sb")
        wq_sb = held.tile([P, DB, D], BF16, name="wq_sb")
        for kb in range(DB):
            nc.sync.dma_start(x_sb[:, kb, 0:CHUNK], x[block(kb), 0:CHUNK])
            nc.sync.dma_start(wq_sb[:, kb, :], wq[block(kb), :])

        def load_weight(w, name):
            w_sb = held.tile([P, DB, D], BF16, name=name)
            nc.sync.dma_start(w_sb[:], w.rearrange("(kb p) m -> p kb m", p=P))
            return w_sb

        def load_along_free_axis(vec, name):
            vec_all = held.tile([P, D], F32, name=name)
            nc.sync.dma_start(vec_all[:], vec.rearrange("d one -> (d one)").partition_broadcast(P))
            return vec_all

        wk_sb = load_weight(wk, "wk_sb")
        wv_sb = load_weight(wv, "wv_sb")
        bv_all = load_along_free_axis(bv, "bv_all")
        nc.sync.dma_start(x_sb[:, :, CHUNK:N], x.rearrange("(kb p) n -> p kb n", p=P)[:, :, CHUNK:N])

        rows = held.tile([P, P], F32, name="rows")
        nc.vector.memset(rows[:], 0.0)
        for i, vec in enumerate((b1, gain, shift)):
            nc.sync.dma_start(rows[i * DB : (i + 1) * DB, :], vec.rearrange("(b p) one -> b (p one)", p=P))

        w1_sb = load_weight(w1, "w1_sb")
        w2_sb = load_weight(w2, "w2_sb")
        b2_all = load_along_free_axis(b2, "b2_all")

        offsets = held.tile([P, N // 16], U16, name="offsets")
        nc.sync.dma_start(offsets[:], offs)
        windows = [held.tile([P, S], F32, name=f"window{b}") for b in range(DB)]
        for b in range(DB):
            nc.sync.dma_start(windows[b][:], base[b * P : (b + 1) * P, :])

        ident_f = held.tile([P, P], F32, name="ident_f")
        make_identity(nc, ident_f[:])
        ident_b = held.tile([P, P], BF16, name="ident_b")
        make_identity(nc, ident_b[:])
        eps_col = held.tile([P, 1], F32, name="eps_col")
        nc.vector.memset(eps_col[:], EPS)

        cols = held.tile([P, 3 * DB], F32, name="cols")

        def rows_to_cols():
            flipped = flip_pool.tile([P, CHUNK], F32, name="flipped")
            nc.tensor.transpose(flipped[:, 0:P], rows[:], ident_f[:])
            nc.vector.tensor_copy(cols[:], flipped[:, 0 : 3 * DB])

        b1_col = [cols[:, b : b + 1] for b in range(DB)]
        gain_col = [cols[:, DB + b : DB + b + 1] for b in range(DB)]
        shift_col = [cols[:, 2 * DB + b : 2 * DB + b + 1] for b in range(DB)]

        q_sb = held.tile([P, DB, N], BF16, name="q_sb")
        k_sb = held.tile([P, DB, N], BF16, name="k_sb")
        vt_sb = held.tile([P, N // L, D], BF16, name="vt_sb")
        y_bf = held.tile([P, DB, N], BF16, name="y_bf")
        r_sb = held.tile([P, DB, N], BF16, name="r_sb")
        y_sb = [held.tile([P, N], F32, name=f"y{b}") for b in range(DB)]
        z_sb = [held.tile([P, N], F32, name=f"z{b}") for b in range(DB)]
        h_sb = held.tile([P, N // L, D], F32, name="h_sb")
        sum_h = held.tile([P, N // L], F32, name="sum_h")
        neg_mean = held.tile([P, N // L], F32, name="neg_mean")
        sum_sq = held.tile([P, N // L], F32, name="sum_sq")
        inv_std = held.tile([P, N // L], F32, name="inv_std")
        neg_mean_scaled = held.tile([P, N // L], F32, name="neg_mean_scaled")

        def project_q(c):
            chunk = slice(c * CHUNK, (c + 1) * CHUNK)
            accs = [acc_pool.tile([P, CHUNK], F32, name="acc") for m in range(DB)]
            for kb in range(DB):
                for m in range(DB):
                    nc.tensor.matmul(accs[m][:], wq_sb[:, kb, block(m)], x_sb[:, kb, chunk], start=(kb == 0), stop=(kb == DB - 1))
            for m in range(DB):
                nc.scalar.activation(q_sb[:, m, chunk], accs[m][:], RELU)

        def project_k(c):
            chunk = slice(c * CHUNK, (c + 1) * CHUNK)
            for m in range(DB):
                acc = acc_pool.tile([P, CHUNK], F32, name="acc")
                for kb in range(DB):
                    nc.tensor.matmul(acc[:], wk_sb[:, kb, block(m)], x_sb[:, kb, chunk], start=(kb == 0), stop=(kb == DB - 1))
                if m % 2 == 0:
                    nc.scalar.activation(k_sb[:, m, chunk], acc[:], RELU)
                else:
                    nc.vector.tensor_scalar_max(k_sb[:, m, chunk], acc[:], 0.0)

        def project_v(u):
            acc = acc_pool.tile([P, D], F32, name="acc")
            for kb in range(DB):
                nc.tensor.matmul(acc[:], x_sb[:, kb, block(u)], wv_sb[:, kb, :], start=(kb == 0), stop=(kb == DB - 1))
            v_pre = work.tile([P, D], BF16, name="v_pre")
            nc.vector.tensor_tensor(v_pre[:], acc[:], bv_all[:], ADD)
            nc.vector.tensor_scalar_max(vt_sb[:, u, :], v_pre[:], 0.0)

        def attention_weights(c):
            scores = attn_pool.tile([P, SEQS, L], F32, name="scores", tag="attn")
            for s in range(SEQS):
                u = c * SEQS + s
                for m in range(DB):
                    nc.tensor.matmul(scores[:, s, :], q_sb[:, m, block(u)], k_sb[:, m, block(u)], start=(m == 0), stop=(m == DB - 1))
            top = small.tile([P, SEQS], F32, name="top")
            nc.vector.reduce_max(top[:], scores[:], mybir.AxisListType.X)
            neg_top = small.tile([P, SEQS], F32, name="neg_top")
            nc.vector.tensor_scalar_mul(neg_top[:], top[:], -1.0 / math.sqrt(D))
            e = work.tile([P, SEQS, L], F32, name="e")
            sums = small.tile([P, SEQS], F32, name="sums")
            for s in range(SEQS):
                nc.scalar.activation(
                    e[:, s, :], scores[:, s, :], EXP, bias=neg_top[:, s : s + 1], scale=1.0 / math.sqrt(D),
                    accum_out=sums[:, s : s + 1],
                )
            inv_sums = small.tile([P, SEQS], F32, name="inv_sums")
            nc.vector.reciprocal(inv_sums[:], sums[:])
            a_bf = work.tile([P, SEQS, L], BF16, name="a_bf")
            for s in range(SEQS):
                nc.vector.tensor_scalar_mul(a_bf[:, s, :], e[:, s, :], inv_sums[:, s : s + 1])
            return a_bf

        def flip_weights(a_bf):
            at_ps = attn_pool.tile([P, SEQS, L], BF16, name="at_ps", tag="attn")
            for s in range(SEQS):
                nc.tensor.transpose(at_ps[:, s, :], a_bf[:, s, :], ident_b[:])
            at_sb = work.tile([P, SEQS, L], BF16, name="at_sb")
            nc.vector.tensor_copy(at_sb[:], at_ps[:])
            return at_sb

        def attend(c, at_sb):
            chunk = slice(c * CHUNK, (c + 1) * CHUNK)
            for b in range(DB):
                acc = acc_pool.tile([P, CHUNK], F32, name="acc")
                for s in range(SEQS):
                    nc.tensor.matmul(acc[:, block(s)], vt_sb[:, c * SEQS + s, block(b)], at_sb[:, s, :], start=True, stop=True)
                nc.vector.tensor_tensor(y_sb[b][:, chunk], acc[:], x_sb[:, b, chunk], ADD)
                nc.scalar.copy(y_bf[:, b, chunk], y_sb[b][:, chunk])

        def feed_forward_hidden(c):
            chunk = slice(c * CHUNK, (c + 1) * CHUNK)
            for m in range(DB):
                acc = acc_pool.tile([P, CHUNK], F32, name="acc")
                for kb in range(DB):
                    nc.tensor.matmul(acc[:], w1_sb[:, kb, block(m)], y_bf[:, kb, chunk], start=(kb == 0), stop=(kb == DB - 1))
                nc.scalar.activation(r_sb[:, m, chunk], acc[:], RELU, bias=b1_col[m])

        def feed_forward_out(u):
            acc = acc_pool.tile([P, D], F32, name="acc")
            for eb in range(DB):
                nc.tensor.matmul(acc[:], r_sb[:, eb, block(u)], w2_sb[:, eb, :], start=(eb == 0), stop=(eb == DB - 1))
            one = slice(u, u + 1)
            nc.vector.scalar_tensor_tensor(h_sb[:, u, :], acc[:], 1.0, b2_all[:], MULT, ADD, accum_out=sum_h[:, one])
            squares = work.tile([P, D], F32, name="squares")
            nc.scalar.activation(
                squares[:], h_sb[:, u, :], SQUARE, bias=sum_h[:, one], scale=-float(D), accum_out=sum_sq[:, one]
            )
            nc.vector.tensor_scalar_mul(neg_mean[:, one], sum_h[:, one], -1.0 / D)

        def feed_forward_out_last(u):
            half = D // 2
            part_sum = small.tile([P, 3], F32, name="part_sum")
            for i, (first, width) in enumerate(((0, half), (half, P), (half + P, P))):
                part = slice(first, first + width)
                acc = acc_pool.tile([P, CHUNK], F32, name="acc")
                for eb in range(DB):
                    nc.tensor.matmul(
                        acc[:, 0:width], r_sb[:, eb, block(u)], w2_sb[:, eb, part], start=(eb == 0), stop=(eb == DB - 1)
                    )
                nc.vector.scalar_tensor_tensor(
                    h_sb[:, u, part], acc[:, 0:width], 1.0, b2_all[:, part], MULT, ADD, accum_out=part_sum[:, i : i + 1]
                )
            sum_0, sum_1, sum_2 = (part_sum[:, i : i + 1] for i in range(3))
            diff_01 = small.tile([P, 1], F32, name="diff_01")
            nc.vector.tensor_tensor(diff_01[:], sum_0, sum_1, SUB)
            sum_01 = small.tile([P, 1], F32, name="sum_01")
            nc.vector.tensor_tensor(sum_01[:], sum_0, sum_1, ADD)
            one = slice(u, u + 1)
            squares = work.tile([P, D], F32, name="squares")
            nc.scalar.activation(
                squares[:], h_sb[:, u, :], SQUARE, bias=sum_0, scale=-float(half), accum_out=sum_sq[:, one]
            )
            mean_gap = small.tile([P, 1], F32, name="mean_gap")
            nc.vector.tensor_scalar(mean_gap[:], sum_2, diff_01[:], 1.0 / D, SUB, MULT)
            gap_sq = small.tile([P, 1], F32, name="gap_sq")
            nc.vector.scalar_tensor_tensor(gap_sq[:], mean_gap[:], mean_gap[:], eps_col[:], MULT, SUB)
            nc.vector.tensor_scalar(neg_mean[:, one], sum_2, sum_01[:], -1.0 / D, ADD, MULT)
            return gap_sq

        def inverse_std_last(u, gap_sq):
            one = slice(u, u + 1)
            nc.scalar.activation(
                inv_std[:, one], sum_sq[:, one], INV_SQRT, bias=gap_sq[:], scale=-1.0 / ((D // 2) ** 2 * D)
            )

        def inverse_std(u):
            one = slice(u, u + 1)
            nc.scalar.activation(inv_std[:, one], sum_sq[:, one], INV_SQRT, bias=eps_col[:], scale=1.0 / D**3)

        def make_first_z(first, count, flipped):
            normed = work.tile([P, SEQS, P], F32, name="normed_first")
            for i in range(count):
                u = first + i
                nc.vector.tensor_scalar(
                    normed[:, i, :], h_sb[:, u, block(0)], neg_mean[:, u : u + 1], inv_std[:, u : u + 1], ADD, MULT
                )
                nc.tensor.transpose(flipped[:, block(i)], normed[:, i, :], ident_f[:])
            for i in range(count):
                nc.vector.tensor_scalar(
                    z_sb[0][:, block(first + i)], flipped[:, block(i)], gain_col[0], shift_col[0], MULT, ADD
                )

        def make_z(b, c):
            normed = work.tile([P, SEQS, P], F32, name="normed")
            flipped = flip_pool.tile([P, CHUNK], F32, name="flipped")
            for s in range(SEQS):
                u = c * SEQS + s
                nc.scalar.activation(
                    normed[:, s, :], h_sb[:, u, block(b)], IDENTITY,
                    bias=neg_mean_scaled[:, u : u + 1], scale=inv_std[:, u : u + 1],
                )
                nc.tensor.transpose(flipped[:, block(s)], normed[:, s, :], ident_f[:])
            nc.scalar.activation(
                z_sb[b][:, c * CHUNK : (c + 1) * CHUNK], flipped[:], IDENTITY, bias=shift_col[b], scale=gain_col[b]
            )

        def place(b):
            nc.vector.tensor_tensor(windows[b][:].indirect(offsets[:]), z_sb[b][:], y_sb[b][:], ADD)
            nc.sync.dma_start(out[b * P : (b + 1) * P, :], windows[b][:])

        project_q(0)
        project_k(0)
        rows_to_cols()
        for u in range(SEQS):
            project_v(u)
        a_bf0 = attention_weights(0)
        project_q(1)
        at_sb0 = flip_weights(a_bf0)
        project_k(1)
        attend(0, at_sb0)
        a_bf1 = attention_weights(1)
        for u in range(SEQS, 2 * SEQS):
            project_v(u)
        at_sb1 = flip_weights(a_bf1)
        feed_forward_hidden(0)
        attend(1, at_sb1)
        for u in range(SEQS - 1):
            feed_forward_out(u)
            inverse_std(u)
        feed_forward_hidden(1)
        feed_forward_out(SEQS - 1)
        inverse_std(SEQS - 1)
        last = N // L - 1
        for u in range(SEQS, last):
            feed_forward_out(u)
            if u < last - 1:
                inverse_std(u)
        gap_sq = feed_forward_out_last(last)
        inverse_std(last - 1)
        inverse_std_last(last, gap_sq)
        make_first_z(0, SEQS, attn_pool.tile([P, CHUNK], F32, name="flipped_first", tag="attn"))
        make_first_z(SEQS, SEQS - 2, flip_pool.tile([P, CHUNK], F32, name="flipped"))
        make_first_z(last - 1, 1, flip_pool.tile([P, CHUNK], F32, name="flipped"))
        make_first_z(last, 1, flip_pool.tile([P, CHUNK], F32, name="flipped"))
        nc.vector.tensor_tensor(neg_mean_scaled[:], neg_mean[:], inv_std[:], MULT)
        place(0)
        for b in range(1, DB):
            make_z(b, 0)
            make_z(b, 1)
            place(b)
